import numpy as np
import ml_dtypes


def mxq(x, axis, fmt="e4m3"):
    dtype, down = {"e4m3": (ml_dtypes.float8_e4m3fn, 7), "e5m2": (ml_dtypes.float8_e5m2, 14)}[fmt]
    v = np.moveaxis(np.asarray(x, np.float32).astype(ml_dtypes.bfloat16).astype(np.float64), axis, -1)
    blocks = v.reshape(v.shape[:-1] + (-1, 32))
    amax = np.abs(blocks).max(-1, keepdims=True)
    byte = np.maximum(np.where(amax > 0, np.frexp(amax)[1] - 1 + 127, 0) - down, 1)
    scale = np.exp2(byte - 127.0)
    codes = (blocks / scale).astype(np.float32).astype(dtype).astype(np.float64)
    return np.moveaxis((codes * scale).reshape(v.shape), -1, axis)


WIDE = False


def mx_kscale(k):
    if not WIDE:
        return np.ones(k)
    levels = np.array([10, -10, 5, -5, 0])
    a = np.random.permutation(np.resize(levels, k // 512 * 4)).reshape(k // 512, 4)
    idx = np.arange(k)
    return np.exp2(a[idx // 512, idx % 128 // 32])


BF16 = ml_dtypes.bfloat16


def bf(x):
    return np.asarray(x, np.float32).astype(BF16)


def f64(x):
    return np.asarray(x).astype(np.float64)


SL, BS, DM, H, NH, DO = 128, 128, 512, 8, 64, 256
DP = H * NH


def setup_inputs():
    s, t = mx_kscale(DM), mx_kscale(DP)
    g = np.random.standard_normal((SL, BS, H)) * 2.0
    return {"values": bf(np.random.standard_normal((SL, BS, DM)) * s),
            "logw": bf(g - np.log(np.exp(g).sum(0, keepdims=True))),
            "Wv": bf(np.random.standard_normal((DP, DM)) / np.sqrt(DM * SL) / s * t[:, None]),
            "Wo": bf(np.random.standard_normal((DO, DP)) * 0.5 / np.sqrt(DP) / t)}


def reference(values, logw, Wv, Wo):
    vp = mxq(f64(values), 2, "e4m3") @ mxq(f64(Wv), 1, "e4m3").T
    attn = (f64(logw)[..., None] * vp.reshape(SL, BS, H, NH)).sum(0)
    return mxq(attn.reshape(BS, DP), 1, "e4m3") @ mxq(f64(Wo), 1, "e4m3").T

@@ -1,0 +1,206 @@
+import concourse.mybir as mybir
+from concourse.masks import make_identity
+
+F32 = mybir.dt.float32
+BF16 = mybir.dt.bfloat16
+U32 = mybir.dt.uint32
+U8 = mybir.dt.uint8
+FP8X4 = mybir.dt.float8_e4m3fn_x4
+MULT = mybir.AluOpType.mult
+ADD = mybir.AluOpType.add
+
+P = 128
+SL, BS, DM, H, NH, DO = 128, 128, 512, 8, 64, 256
+DP = H * NH
+PACK = 4
+WORDS = DM // 2
+GROUP = 4
+N_GROUPS = SL // GROUP
+WO_GROUP = 3
+
+FLOPS = 2 * SL * BS * DM * DP + 2 * BS * DP * DO
+
+
+def tile_multiheadattention_pb_t_kernel(tc, values, logw, Wv, Wo, out):
+    nc = tc.nc
+    with tc.tile_pool(name="const", bufs=1) as const, tc.tile_pool(
+        name="rows", bufs=N_GROUPS
+    ) as rows_pool, tc.tile_pool(name="work", bufs=3) as work, tc.psum_pool(
+        name="flip", bufs=2
+    ) as flip_pool, tc.psum_pool(name="proj", bufs=5) as proj_pool, tc.manual_schedule():
+
+        def pairs_onto_partitions(src_words, dst_words):
+            bank = flip_pool.tile([P, 2, 2, P], F32, tag="flip")
+            for blk in range(2):
+                for u in range(2):
+                    nc.tensor.transpose(
+                        bank[:, blk, u, :], src_words[:, blk, u * P : (u + 1) * P], ident[:]
+                    )
+            nc.scalar.copy(out=dst_words, in_=bank[:].rearrange("p k u r -> p k r u"))
+
+        wv_rows = const.tile([P, 4 * DM], BF16)
+        nc.sync.dma_start(
+            out=wv_rows[:].rearrange("p (t k) -> p t k", k=DM),
+            in_=Wv.rearrange("(t p) k -> p t k", p=P),
+        )
+        logw_rows = const.tile([P, BS * H], BF16)
+        nc.scalar.dma_start(out=logw_rows[:], in_=logw.rearrange("s b h -> s (b h)"))
+        wo_rows = const.tile([P, 2 * DP], BF16)
+        nc.scalar.dma_start(
+            out=wo_rows[:].rearrange("p (i c) -> p i c", c=DP),
+            in_=Wo.rearrange("(i p) c -> p i c", p=P),
+        )
+        value_rows = []
+        for g in range(N_GROUPS):
+            rows = rows_pool.tile([P, GROUP * DM], BF16)
+            nc.sync.dma_start(
+                out=rows[:].rearrange("b (s k) -> b s k", k=DM),
+                in_=values[g * GROUP : (g + 1) * GROUP].rearrange("s b k -> b s k"),
+            )
+            value_rows.append(rows)
+
+        ident = const.tile([P, P], F32)
+        make_identity(nc, ident[:])
+        attn = const.tile([P, DP], F32)
+        nc.vector.memset(attn[:], 0.0)
+
+        logw_by_head = const.tile([P, H, BS], F32)
+        nc.vector.tensor_copy(
+            out=logw_by_head[:], in_=logw_rows[:].rearrange("s (b h) -> s h b", h=H)
+        )
+        weight = const.tile([P, H, SL], F32)
+
+        wv_grouped = const.tile([P, DP * PACK], BF16, align_bytes=64)
+        wv_codes = const.tile([P, DP], U32, align_bytes=64)
+        wv_scales = const.tile([P, DP], U8, align_bytes=64)
+        wv_words = wv_rows[:].bitcast(F32).rearrange("p (t w) -> p t w", w=WORDS)
+        wv_grouped_words = wv_grouped[:].bitcast(F32).rearrange("p (t c u) -> p t c u", c=P, u=2)
+        for half in range(2):
+            pairs_onto_partitions(
+                wv_words[:, 2 * half : 2 * half + 2, :],
+                wv_grouped_words[:, 2 * half : 2 * half + 2, :, :],
+            )
+        nc.vector.quantize_mx(
+            out=wv_codes[:].bitcast(FP8X4), scales=wv_scales[:], in_=wv_grouped[:]
+        )
+
+        def prepare_weight():
+            for half in range(2):
+                bank = flip_pool.tile([P, 4, P], F32, tag="flip")
+                for i in range(4):
+                    nc.tensor.transpose(bank[:, i, :], logw_by_head[:, 4 * half + i, :], ident[:])
+                nc.scalar.copy(out=weight[:, 4 * half : 4 * half + 4, :], in_=bank[:])
+
+        def prepare_wo():
+            wo_f32 = const.tile([P, 2, DP], F32)
+            nc.scalar.copy(out=wo_f32[:], in_=wo_rows[:].rearrange("p (i c) -> p i c", c=DP))
+            for i in range(2):
+                bank = flip_pool.tile([P, PACK, P], F32, tag="flip")
+                for t in range(PACK):
+                    nc.tensor.transpose(bank[:, t, :], wo_f32[:, i, t * P : (t + 1) * P], ident[:])
+                nc.scalar.copy(
+                    out=wo_grouped[:, i * P : (i + 1) * P, :],
+                    in_=bank[:].rearrange("p t o -> p o t"),
+                )
+            nc.vector.quantize_mx(
+                out=wo_codes[:].bitcast(FP8X4),
+                scales=wo_scales[:],
+                in_=wo_grouped[:].rearrange("p o t -> p (o t)"),
+            )
+
+        wo_grouped = const.tile([P, DO, PACK], BF16, align_bytes=64)
+        wo_codes = const.tile([P, DO], U32, align_bytes=64)
+        wo_scales = const.tile([P, DO], U8, align_bytes=64)
+
+        grouped_of = {}
+        codes_of = {}
+        scales_of = {}
+        proj_of = {}
+
+        def flip_group(g):
+            grouped = work.tile([P, GROUP * BS * PACK], BF16, align_bytes=64)
+            src = value_rows[g][:].bitcast(F32).rearrange("b (s w) -> b s w", w=WORDS)
+            dst = grouped[:].bitcast(F32).rearrange("p (s b u) -> p s b u", b=BS, u=2)
+            for pair in range(GROUP // 2):
+                pairs_onto_partitions(
+                    src[:, 2 * pair : 2 * pair + 2, :], dst[:, 2 * pair : 2 * pair + 2, :, :]
+                )
+            grouped_of[g] = grouped
+
+        def quantise_group(g):
+            codes = work.tile([P, GROUP * BS], U32, align_bytes=64)
+            scales = work.tile([P, GROUP * BS], U8, align_bytes=64)
+            nc.vector.quantize_mx(
+                out=codes[:].bitcast(FP8X4), scales=scales[:], in_=grouped_of[g][:]
+            )
+            codes_of[g] = codes
+            scales_of[g] = scales
+
+        def project_group(g):
+            codes = codes_of[g]
+            scales = scales_of[g]
+            for j in range(GROUP):
+                proj = proj_pool.tile([P, DP], F32)
+                nc.tensor.matmul_mx(
+                    out=proj[:],
+                    lhsT=codes[:, j * BS : (j + 1) * BS].bitcast(FP8X4),
+                    lhsT_scale=scales[:, j * BS : (j + 1) * BS],
+                    rhs=wv_codes[:].bitcast(FP8X4),
+                    rhs_scale=wv_scales[:],
+                    start=True,
+                    stop=True,
+                )
+                proj_of[g * GROUP + j] = proj
+
+        def pool_group(g):
+            for s in range(g * GROUP, (g + 1) * GROUP):
+                for h in range(H):
+                    head = slice(h * NH, (h + 1) * NH)
+                    nc.vector.scalar_tensor_tensor(
+                        out=attn[:, head],
+                        in0=proj_of[s][:, head],
+                        scalar=weight[:, h, s : s + 1],
+                        in1=attn[:, head],
+                        op0=MULT,
+                        op1=ADD,
+                    )
+
+        flip_group(0)
+        prepare_weight()
+        for g in range(1, N_GROUPS + 2):
+            if g < N_GROUPS:
+                flip_group(g)
+            if g == WO_GROUP:
+                prepare_wo()
+            if g <= N_GROUPS:
+                quantise_group(g - 1)
+            if g >= 2:
+                pool_group(g - 2)
+            if g <= N_GROUPS:
+                project_group(g - 1)
+
+        attn_bank = flip_pool.tile([P, PACK, BS], F32, tag="flip")
+        for t in range(PACK):
+            nc.tensor.transpose(attn_bank[:, t, :], attn[:, t * P : (t + 1) * P], ident[:])
+        attn_grouped = const.tile([P, BS, PACK], BF16, align_bytes=64)
+        nc.scalar.copy(out=attn_grouped[:], in_=attn_bank[:].rearrange("p t b -> p b t"))
+        attn_codes = const.tile([P, BS], U32, align_bytes=64)
+        attn_scales = const.tile([P, BS], U8, align_bytes=64)
+        nc.vector.quantize_mx(
+            out=attn_codes[:].bitcast(FP8X4),
+            scales=attn_scales[:],
+            in_=attn_grouped[:].rearrange("p b t -> p (b t)"),
+        )
+        out_bank = flip_pool.tile([P, DO], F32, tag="flip")
+        nc.tensor.matmul_mx(
+            out=out_bank[:],
+            lhsT=attn_codes[:].bitcast(FP8X4),
+            lhsT_scale=attn_scales[:],
+            rhs=wo_codes[:].bitcast(FP8X4),
+            rhs_scale=wo_scales[:],
+            start=True,
+            stop=True,
+        )
+        out_rows = const.tile([P, DO], F32)
+        nc.vector.tensor_copy(out=out_rows[:], in_=out_bank[:])
+        nc.sync.dma_start(out=out, in_=out_rows[:])

@@ -8,6 +8,7 @@ U8 = mybir.dt.uint8
 FP8X4 = mybir.dt.float8_e4m3fn_x4
 MULT = mybir.AluOpType.mult
 ADD = mybir.AluOpType.add
+COPY = mybir.ActivationFunctionType.Copy
 
 P = 128
 SL, BS, DM, H, NH, DO = 128, 128, 512, 8, 64, 256
@@ -17,6 +18,7 @@ WORDS = DM // 2
 GROUP = 4
 N_GROUPS = SL // GROUP
 WO_GROUP = 3
+SCALAR_EVERY = 3
 
 FLOPS = 2 * SL * BS * DM * DP + 2 * BS * DP * DO
 
@@ -27,7 +29,9 @@ def tile_multiheadattention_pb_t_kernel(tc, values, logw, Wv, Wo, out):
         name="rows", bufs=N_GROUPS
     ) as rows_pool, tc.tile_pool(name="work", bufs=3) as work, tc.psum_pool(
         name="flip", bufs=2
-    ) as flip_pool, tc.psum_pool(name="proj", bufs=5) as proj_pool, tc.manual_schedule():
+    ) as flip_pool, tc.psum_pool(name="proj", bufs=5) as proj_pool, tc.psum_pool(
+        name="sum", bufs=1
+    ) as sum_pool, tc.tile_pool(name="prod", bufs=4) as prod_pool, tc.manual_schedule():
 
         def pairs_onto_partitions(src_words, dst_words):
             bank = flip_pool.tile([P, 2, 2, P], F32, tag="flip")
@@ -116,6 +120,7 @@ def tile_multiheadattention_pb_t_kernel(tc, values, logw, Wv, Wo, out):
         codes_of = {}
         scales_of = {}
         proj_of = {}
+        product_of = {}
 
         def flip_group(g):
             grouped = work.tile([P, GROUP * BS * PACK], BF16, align_bytes=64)
@@ -152,38 +157,70 @@ def tile_multiheadattention_pb_t_kernel(tc, values, logw, Wv, Wo, out):
                 )
                 proj_of[g * GROUP + j] = proj
 
+        def by_scalar(s):
+            return s % SCALAR_EVERY == SCALAR_EVERY - 1
+
         def pool_group(g):
             for s in range(g * GROUP, (g + 1) * GROUP):
+                if by_scalar(s):
+                    product = prod_pool.tile([P, DP], F32)
+                    product_of[s] = product
                 for h in range(H):
                     head = slice(h * NH, (h + 1) * NH)
-                    nc.vector.scalar_tensor_tensor(
-                        out=attn[:, head],
-                        in0=proj_of[s][:, head],
-                        scalar=weight[:, h, s : s + 1],
-                        in1=attn[:, head],
-                        op0=MULT,
-                        op1=ADD,
-                    )
+                    if by_scalar(s):
+                        nc.scalar.activation(
+                            out=product[:, head],
+                            in_=proj_of[s][:, head],
+                            func=COPY,
+                            scale=weight[:, h, s : s + 1],
+                        )
+                    else:
+                        nc.vector.scalar_tensor_tensor(
+                            out=attn[:, head],
+                            in0=proj_of[s][:, head],
+                            scalar=weight[:, h, s : s + 1],
+                            in1=attn[:, head],
+                            op0=MULT,
+                            op1=ADD,
+                        )
+
+        attn_sum = sum_pool.tile([P, PACK, BS], F32)
+
+        def add_transposed(term, first, last):
+            for t in range(PACK):
+                nc.tensor.matmul(
+                    out=attn_sum[:, t, :],
+                    lhsT=term[:, t * P : (t + 1) * P],
+                    rhs=ident[:],
+                    is_transpose=True,
+                    start=first and t == 0,
+                    stop=last and t == PACK - 1,
+                )
+
+        def add_products_of_group(g):
+            for s in range(g * GROUP, (g + 1) * GROUP):
+                if by_scalar(s):
+                    add_transposed(product_of[s], first=(s == SCALAR_EVERY - 1), last=False)
 
         flip_group(0)
         prepare_weight()
-        for g in range(1, N_GROUPS + 2):
+        for g in range(1, N_GROUPS + 3):
             if g < N_GROUPS:
                 flip_group(g)
+            if g >= 3:
+                add_products_of_group(g - 3)
             if g == WO_GROUP:
                 prepare_wo()
             if g <= N_GROUPS:
                 quantise_group(g - 1)
-            if g >= 2:
+            if 2 <= g <= N_GROUPS + 1:
                 pool_group(g - 2)
             if g <= N_GROUPS:
                 project_group(g - 1)
 
-        attn_bank = flip_pool.tile([P, PACK, BS], F32, tag="flip")
-        for t in range(PACK):
-            nc.tensor.transpose(attn_bank[:, t, :], attn[:, t * P : (t + 1) * P], ident[:])
+        add_transposed(attn, first=False, last=True)
         attn_grouped = const.tile([P, BS, PACK], BF16, align_bytes=64)
-        nc.scalar.copy(out=attn_grouped[:], in_=attn_bank[:].rearrange("p t b -> p b t"))
+        nc.scalar.copy(out=attn_grouped[:], in_=attn_sum[:].rearrange("p t b -> p b t"))
         attn_codes = const.tile([P, BS], U32, align_bytes=64)
         attn_scales = const.tile([P, BS], U8, align_bytes=64)
         nc.vector.quantize_mx(

@@ -204,17 +204,18 @@ def tile_multiheadattention_pb_t_kernel(tc, values, logw, Wv, Wo, out):
 
         flip_group(0)
         prepare_weight()
+        flip_group(1)
         for g in range(1, N_GROUPS + 3):
-            if g < N_GROUPS:
-                flip_group(g)
-            if g >= 3:
-                add_products_of_group(g - 3)
-            if g == WO_GROUP:
-                prepare_wo()
             if g <= N_GROUPS:
                 quantise_group(g - 1)
             if 2 <= g <= N_GROUPS + 1:
                 pool_group(g - 2)
+            if g + 1 < N_GROUPS:
+                flip_group(g + 1)
+            if g >= 3:
+                add_products_of_group(g - 3)
+            if g == WO_GROUP:
+                prepare_wo()
             if g <= N_GROUPS:
                 project_group(g - 1)
 

@@ -18,7 +18,7 @@ WORDS = DM // 2
 GROUP = 4
 N_GROUPS = SL // GROUP
 WO_GROUP = 3
-SCALAR_EVERY = 3
+SCALAR_SHARE, SHARE_OF = 4, 11
 
 FLOPS = 2 * SL * BS * DM * DP + 2 * BS * DP * DO
 
@@ -106,6 +106,8 @@ def tile_multiheadattention_pb_t_kernel(tc, values, logw, Wv, Wo, out):
                     out=wo_grouped[:, i * P : (i + 1) * P, :],
                     in_=bank[:].rearrange("p t o -> p o t"),
                 )
+
+        def quantise_wo():
             nc.vector.quantize_mx(
                 out=wo_codes[:].bitcast(FP8X4),
                 scales=wo_scales[:],
@@ -158,7 +160,7 @@ def tile_multiheadattention_pb_t_kernel(tc, values, logw, Wv, Wo, out):
                 proj_of[g * GROUP + j] = proj
 
         def by_scalar(s):
-            return s % SCALAR_EVERY == SCALAR_EVERY - 1
+            return (s * SCALAR_SHARE) % SHARE_OF < SCALAR_SHARE
 
         def pool_group(g):
             for s in range(g * GROUP, (g + 1) * GROUP):
@@ -200,7 +202,7 @@ def tile_multiheadattention_pb_t_kernel(tc, values, logw, Wv, Wo, out):
         def add_products_of_group(g):
             for s in range(g * GROUP, (g + 1) * GROUP):
                 if by_scalar(s):
-                    add_transposed(product_of[s], first=(s == SCALAR_EVERY - 1), last=False)
+                    add_transposed(product_of[s], first=(s == 0), last=False)
 
         flip_group(0)
         prepare_weight()
@@ -208,6 +210,8 @@ def tile_multiheadattention_pb_t_kernel(tc, values, logw, Wv, Wo, out):
         for g in range(1, N_GROUPS + 3):
             if g <= N_GROUPS:
                 quantise_group(g - 1)
+            if g == WO_GROUP + 1:
+                quantise_wo()
             if 2 <= g <= N_GROUPS + 1:
                 pool_group(g - 2)
             if g + 1 < N_GROUPS:

@@ -14,11 +14,11 @@ P = 128
 SL, BS, DM, H, NH, DO = 128, 128, 512, 8, 64, 256
 DP = H * NH
 PACK = 4
-WORDS = DM // 2
+PAIRS = DM // 2
 GROUP = 4
 N_GROUPS = SL // GROUP
-WO_GROUP = 3
-SCALAR_SHARE, SHARE_OF = 4, 11
+SCALAR_EVERY = 3
+WO_ROUND = 3
 
 FLOPS = 2 * SL * BS * DM * DP + 2 * BS * DP * DO
 
@@ -27,21 +27,11 @@ def tile_multiheadattention_pb_t_kernel(tc, values, logw, Wv, Wo, out):
     nc = tc.nc
     with tc.tile_pool(name="const", bufs=1) as const, tc.tile_pool(
         name="rows", bufs=N_GROUPS
-    ) as rows_pool, tc.tile_pool(name="work", bufs=3) as work, tc.psum_pool(
-        name="flip", bufs=2
-    ) as flip_pool, tc.psum_pool(name="proj", bufs=5) as proj_pool, tc.psum_pool(
-        name="sum", bufs=1
-    ) as sum_pool, tc.tile_pool(name="prod", bufs=4) as prod_pool, tc.manual_schedule():
-
-        def pairs_onto_partitions(src_words, dst_words):
-            bank = flip_pool.tile([P, 2, 2, P], F32, tag="flip")
-            for blk in range(2):
-                for u in range(2):
-                    nc.tensor.transpose(
-                        bank[:, blk, u, :], src_words[:, blk, u * P : (u + 1) * P], ident[:]
-                    )
-            nc.scalar.copy(out=dst_words, in_=bank[:].rearrange("p k u r -> p k r u"))
-
+    ) as rows_pool, tc.tile_pool(name="work", bufs=3) as work_pool, tc.tile_pool(
+        name="prod", bufs=4
+    ) as prod_pool, tc.psum_pool(name="flip", bufs=2) as flip_pool, tc.psum_pool(
+        name="proj", bufs=5
+    ) as proj_pool, tc.psum_pool(name="sum", bufs=1) as sum_pool, tc.manual_schedule():
         wv_rows = const.tile([P, 4 * DM], BF16)
         nc.sync.dma_start(
             out=wv_rows[:].rearrange("p (t k) -> p t k", k=DM),
@@ -49,11 +39,8 @@ def tile_multiheadattention_pb_t_kernel(tc, values, logw, Wv, Wo, out):
         )
         logw_rows = const.tile([P, BS * H], BF16)
         nc.scalar.dma_start(out=logw_rows[:], in_=logw.rearrange("s b h -> s (b h)"))
-        wo_rows = const.tile([P, 2 * DP], BF16)
-        nc.scalar.dma_start(
-            out=wo_rows[:].rearrange("p (i c) -> p i c", c=DP),
-            in_=Wo.rearrange("(i p) c -> p i c", p=P),
-        )
+        wo_rows = const.tile([P, 2, DP], BF16)
+        nc.scalar.dma_start(out=wo_rows[:], in_=Wo.rearrange("(i p) c -> p i c", p=P))
         value_rows = []
         for g in range(N_GROUPS):
             rows = rows_pool.tile([P, GROUP * DM], BF16)
@@ -65,43 +52,61 @@ def tile_multiheadattention_pb_t_kernel(tc, values, logw, Wv, Wo, out):
 
         ident = const.tile([P, P], F32)
         make_identity(nc, ident[:])
-        attn = const.tile([P, DP], F32)
-        nc.vector.memset(attn[:], 0.0)
+        ident_bf16 = const.tile([P, P], BF16)
+        nc.vector.tensor_copy(out=ident_bf16[:], in_=ident[:])
+
+        def pairs_onto_partitions(src_pairs, dst_pairs):
+            bank = flip_pool.tile([P, 2, 2, P], F32, tag="flip")
+            for blk in range(2):
+                for u in range(2):
+                    nc.tensor.transpose(
+                        bank[:, blk, u, :], src_pairs[:, blk, u * P : (u + 1) * P], ident[:]
+                    )
+            nc.scalar.copy(out=dst_pairs, in_=bank[:].rearrange("p k u r -> p k r u"))
 
         logw_by_head = const.tile([P, H, BS], F32)
         nc.vector.tensor_copy(
             out=logw_by_head[:], in_=logw_rows[:].rearrange("s (b h) -> s h b", h=H)
         )
-        weight = const.tile([P, H, SL], F32)
 
         wv_grouped = const.tile([P, DP * PACK], BF16, align_bytes=64)
         wv_codes = const.tile([P, DP], U32, align_bytes=64)
         wv_scales = const.tile([P, DP], U8, align_bytes=64)
-        wv_words = wv_rows[:].bitcast(F32).rearrange("p (t w) -> p t w", w=WORDS)
-        wv_grouped_words = wv_grouped[:].bitcast(F32).rearrange("p (t c u) -> p t c u", c=P, u=2)
+        wv_pairs = wv_rows[:].bitcast(F32).rearrange("p (t w) -> p t w", w=PAIRS)
+        wv_grouped_pairs = wv_grouped[:].bitcast(F32).rearrange("p (t c u) -> p t c u", c=P, u=2)
         for half in range(2):
             pairs_onto_partitions(
-                wv_words[:, 2 * half : 2 * half + 2, :],
-                wv_grouped_words[:, 2 * half : 2 * half + 2, :, :],
+                wv_pairs[:, 2 * half : 2 * half + 2, :],
+                wv_grouped_pairs[:, 2 * half : 2 * half + 2, :, :],
             )
         nc.vector.quantize_mx(
             out=wv_codes[:].bitcast(FP8X4), scales=wv_scales[:], in_=wv_grouped[:]
         )
 
-        def prepare_weight():
-            for half in range(2):
-                bank = flip_pool.tile([P, 4, P], F32, tag="flip")
-                for i in range(4):
-                    nc.tensor.transpose(bank[:, i, :], logw_by_head[:, 4 * half + i, :], ident[:])
-                nc.scalar.copy(out=weight[:, 4 * half : 4 * half + 4, :], in_=bank[:])
+        weight = const.tile([P, H, SL], F32)
 
-        def prepare_wo():
-            wo_f32 = const.tile([P, 2, DP], F32)
-            nc.scalar.copy(out=wo_f32[:], in_=wo_rows[:].rearrange("p (i c) -> p i c", c=DP))
-            for i in range(2):
-                bank = flip_pool.tile([P, PACK, P], F32, tag="flip")
+        def transpose_logw():
+            for half in range(2):
+                bank = flip_pool.tile([P, H // 2, SL], F32, tag="flip")
+                for i in range(H // 2):
+                    nc.tensor.transpose(
+                        bank[:, i, :], logw_by_head[:, half * (H // 2) + i, :], ident[:]
+                    )
+                nc.scalar.copy(
+                    out=weight[:, half * (H // 2) : (half + 1) * (H // 2), :], in_=bank[:]
+                )
+
+        wo_grouped = const.tile([P, DO, PACK], BF16, align_bytes=64)
+        wo_codes = const.tile([P, DO], U32, align_bytes=64)
+        wo_scales = const.tile([P, DO], U8, align_bytes=64)
+
+        def transpose_wo():
+            for i in range(DO // P):
+                bank = flip_pool.tile([P, PACK, P], BF16, tag="flip")
                 for t in range(PACK):
-                    nc.tensor.transpose(bank[:, t, :], wo_f32[:, i, t * P : (t + 1) * P], ident[:])
+                    nc.tensor.transpose(
+                        bank[:, t, :], wo_rows[:, i, t * P : (t + 1) * P], ident_bf16[:]
+                    )
                 nc.scalar.copy(
                     out=wo_grouped[:, i * P : (i + 1) * P, :],
                     in_=bank[:].rearrange("p t o -> p o t"),
@@ -114,29 +119,25 @@ def tile_multiheadattention_pb_t_kernel(tc, values, logw, Wv, Wo, out):
                 in_=wo_grouped[:].rearrange("p o t -> p (o t)"),
             )
 
-        wo_grouped = const.tile([P, DO, PACK], BF16, align_bytes=64)
-        wo_codes = const.tile([P, DO], U32, align_bytes=64)
-        wo_scales = const.tile([P, DO], U8, align_bytes=64)
-
         grouped_of = {}
         codes_of = {}
         scales_of = {}
         proj_of = {}
         product_of = {}
 
-        def flip_group(g):
-            grouped = work.tile([P, GROUP * BS * PACK], BF16, align_bytes=64)
-            src = value_rows[g][:].bitcast(F32).rearrange("b (s w) -> b s w", w=WORDS)
+        def transpose_group(g):
+            grouped = work_pool.tile([P, GROUP * BS * PACK], BF16, align_bytes=64)
+            src = value_rows[g][:].bitcast(F32).rearrange("b (s w) -> b s w", w=PAIRS)
             dst = grouped[:].bitcast(F32).rearrange("p (s b u) -> p s b u", b=BS, u=2)
-            for pair in range(GROUP // 2):
+            for half in range(GROUP // 2):
                 pairs_onto_partitions(
-                    src[:, 2 * pair : 2 * pair + 2, :], dst[:, 2 * pair : 2 * pair + 2, :, :]
+                    src[:, 2 * half : 2 * half + 2, :], dst[:, 2 * half : 2 * half + 2, :, :]
                 )
             grouped_of[g] = grouped
 
         def quantise_group(g):
-            codes = work.tile([P, GROUP * BS], U32, align_bytes=64)
-            scales = work.tile([P, GROUP * BS], U8, align_bytes=64)
+            codes = work_pool.tile([P, GROUP * BS], U32, align_bytes=64)
+            scales = work_pool.tile([P, GROUP * BS], U8, align_bytes=64)
             nc.vector.quantize_mx(
                 out=codes[:].bitcast(FP8X4), scales=scales[:], in_=grouped_of[g][:]
             )
@@ -144,14 +145,13 @@ def tile_multiheadattention_pb_t_kernel(tc, values, logw, Wv, Wo, out):
             scales_of[g] = scales
 
         def project_group(g):
-            codes = codes_of[g]
-            scales = scales_of[g]
             for j in range(GROUP):
+                batch = slice(j * BS, (j + 1) * BS)
                 proj = proj_pool.tile([P, DP], F32)
                 nc.tensor.matmul_mx(
                     out=proj[:],
-                    lhsT=codes[:, j * BS : (j + 1) * BS].bitcast(FP8X4),
-                    lhsT_scale=scales[:, j * BS : (j + 1) * BS],
+                    lhsT=codes_of[g][:, batch].bitcast(FP8X4),
+                    lhsT_scale=scales_of[g][:, batch],
                     rhs=wv_codes[:].bitcast(FP8X4),
                     rhs_scale=wv_scales[:],
                     start=True,
@@ -160,7 +160,10 @@ def tile_multiheadattention_pb_t_kernel(tc, values, logw, Wv, Wo, out):
                 proj_of[g * GROUP + j] = proj
 
         def by_scalar(s):
-            return (s * SCALAR_SHARE) % SHARE_OF < SCALAR_SHARE
+            return s % SCALAR_EVERY == SCALAR_EVERY - 1
+
+        attn_part = const.tile([P, DP], F32)
+        nc.vector.memset(attn_part[:], 0.0)
 
         def pool_group(g):
             for s in range(g * GROUP, (g + 1) * GROUP):
@@ -178,10 +181,10 @@ def tile_multiheadattention_pb_t_kernel(tc, values, logw, Wv, Wo, out):
                         )
                     else:
                         nc.vector.scalar_tensor_tensor(
-                            out=attn[:, head],
+                            out=attn_part[:, head],
                             in0=proj_of[s][:, head],
                             scalar=weight[:, h, s : s + 1],
-                            in1=attn[:, head],
+                            in1=attn_part[:, head],
                             op0=MULT,
                             op1=ADD,
                         )
@@ -202,28 +205,28 @@ def tile_multiheadattention_pb_t_kernel(tc, values, logw, Wv, Wo, out):
         def add_products_of_group(g):
             for s in range(g * GROUP, (g + 1) * GROUP):
                 if by_scalar(s):
-                    add_transposed(product_of[s], first=(s == 0), last=False)
+                    add_transposed(product_of[s], first=(s == SCALAR_EVERY - 1), last=False)
 
-        flip_group(0)
-        prepare_weight()
-        flip_group(1)
+        transpose_group(0)
+        transpose_logw()
+        transpose_group(1)
         for g in range(1, N_GROUPS + 3):
             if g <= N_GROUPS:
                 quantise_group(g - 1)
-            if g == WO_GROUP + 1:
+            if g == WO_ROUND + 1:
                 quantise_wo()
             if 2 <= g <= N_GROUPS + 1:
                 pool_group(g - 2)
             if g + 1 < N_GROUPS:
-                flip_group(g + 1)
+                transpose_group(g + 1)
             if g >= 3:
                 add_products_of_group(g - 3)
-            if g == WO_GROUP:
-                prepare_wo()
+            if g == WO_ROUND:
+                transpose_wo()
             if g <= N_GROUPS:
                 project_group(g - 1)
 
-        add_transposed(attn, first=False, last=True)
+        add_transposed(attn_part, first=False, last=True)
         attn_grouped = const.tile([P, BS, PACK], BF16, align_bytes=64)
         nc.scalar.copy(out=attn_grouped[:], in_=attn_sum[:].rearrange("p t b -> p b t"))
         attn_codes = const.tile([P, BS], U32, align_bytes=64)

import concourse.mybir as mybir
from concourse.masks import make_identity

F32 = mybir.dt.float32
BF16 = mybir.dt.bfloat16
U32 = mybir.dt.uint32
U8 = mybir.dt.uint8
FP8X4 = mybir.dt.float8_e4m3fn_x4
MULT = mybir.AluOpType.mult
ADD = mybir.AluOpType.add
COPY = mybir.ActivationFunctionType.Copy

P = 128
SL, BS, DM, H, NH, DO = 128, 128, 512, 8, 64, 256
DP = H * NH
PACK = 4
PAIRS = DM // 2
GROUP = 4
N_GROUPS = SL // GROUP
SCALAR_EVERY = 3
WO_ROUND = 3

FLOPS = 2 * SL * BS * DM * DP + 2 * BS * DP * DO


def tile_multiheadattention_pb_t_kernel(tc, values, logw, Wv, Wo, out):
    nc = tc.nc
    with tc.tile_pool(name="const", bufs=1) as const, tc.tile_pool(
        name="rows", bufs=N_GROUPS
    ) as rows_pool, tc.tile_pool(name="work", bufs=3) as work_pool, tc.tile_pool(
        name="prod", bufs=4
    ) as prod_pool, tc.psum_pool(name="flip", bufs=2) as flip_pool, tc.psum_pool(
        name="proj", bufs=5
    ) as proj_pool, tc.psum_pool(name="sum", bufs=1) as sum_pool, tc.manual_schedule():
        wv_rows = const.tile([P, 4 * DM], BF16)
        nc.sync.dma_start(
            out=wv_rows[:].rearrange("p (t k) -> p t k", k=DM),
            in_=Wv.rearrange("(t p) k -> p t k", p=P),
        )
        logw_rows = const.tile([P, BS * H], BF16)
        nc.scalar.dma_start(out=logw_rows[:], in_=logw.rearrange("s b h -> s (b h)"))
        wo_rows = const.tile([P, 2, DP], BF16)
        nc.scalar.dma_start(out=wo_rows[:], in_=Wo.rearrange("(i p) c -> p i c", p=P))
        value_rows = []
        for g in range(N_GROUPS):
            rows = rows_pool.tile([P, GROUP * DM], BF16)
            nc.sync.dma_start(
                out=rows[:].rearrange("b (s k) -> b s k", k=DM),
                in_=values[g * GROUP : (g + 1) * GROUP].rearrange("s b k -> b s k"),
            )
            value_rows.append(rows)

        ident = const.tile([P, P], F32)
        make_identity(nc, ident[:])
        ident_bf16 = const.tile([P, P], BF16)
        nc.vector.tensor_copy(out=ident_bf16[:], in_=ident[:])

        def pairs_onto_partitions(src_pairs, dst_pairs):
            bank = flip_pool.tile([P, 2, 2, P], F32, tag="flip")
            for blk in range(2):
                for u in range(2):
                    nc.tensor.transpose(
                        bank[:, blk, u, :], src_pairs[:, blk, u * P : (u + 1) * P], ident[:]
                    )
            nc.scalar.copy(out=dst_pairs, in_=bank[:].rearrange("p k u r -> p k r u"))

        logw_by_head = const.tile([P, H, BS], F32)
        nc.vector.tensor_copy(
            out=logw_by_head[:], in_=logw_rows[:].rearrange("s (b h) -> s h b", h=H)
        )

        wv_grouped = const.tile([P, DP * PACK], BF16, align_bytes=64)
        wv_codes = const.tile([P, DP], U32, align_bytes=64)
        wv_scales = const.tile([P, DP], U8, align_bytes=64)
        wv_pairs = wv_rows[:].bitcast(F32).rearrange("p (t w) -> p t w", w=PAIRS)
        wv_grouped_pairs = wv_grouped[:].bitcast(F32).rearrange("p (t c u) -> p t c u", c=P, u=2)
        for half in range(2):
            pairs_onto_partitions(
                wv_pairs[:, 2 * half : 2 * half + 2, :],
                wv_grouped_pairs[:, 2 * half : 2 * half + 2, :, :],
            )
        nc.vector.quantize_mx(
            out=wv_codes[:].bitcast(FP8X4), scales=wv_scales[:], in_=wv_grouped[:]
        )

        weight = const.tile([P, H, SL], F32)

        def transpose_logw():
            for half in range(2):
                bank = flip_pool.tile([P, H // 2, SL], F32, tag="flip")
                for i in range(H // 2):
                    nc.tensor.transpose(
                        bank[:, i, :], logw_by_head[:, half * (H // 2) + i, :], ident[:]
                    )
                nc.scalar.copy(
                    out=weight[:, half * (H // 2) : (half + 1) * (H // 2), :], in_=bank[:]
                )

        wo_grouped = const.tile([P, DO, PACK], BF16, align_bytes=64)
        wo_codes = const.tile([P, DO], U32, align_bytes=64)
        wo_scales = const.tile([P, DO], U8, align_bytes=64)

        def transpose_wo():
            for i in range(DO // P):
                bank = flip_pool.tile([P, PACK, P], BF16, tag="flip")
                for t in range(PACK):
                    nc.tensor.transpose(
                        bank[:, t, :], wo_rows[:, i, t * P : (t + 1) * P], ident_bf16[:]
                    )
                nc.scalar.copy(
                    out=wo_grouped[:, i * P : (i + 1) * P, :],
                    in_=bank[:].rearrange("p t o -> p o t"),
                )

        def quantise_wo():
            nc.vector.quantize_mx(
                out=wo_codes[:].bitcast(FP8X4),
                scales=wo_scales[:],
                in_=wo_grouped[:].rearrange("p o t -> p (o t)"),
            )

        grouped_of = {}
        codes_of = {}
        scales_of = {}
        proj_of = {}
        product_of = {}

        def transpose_group(g):
            grouped = work_pool.tile([P, GROUP * BS * PACK], BF16, align_bytes=64)
            src = value_rows[g][:].bitcast(F32).rearrange("b (s w) -> b s w", w=PAIRS)
            dst = grouped[:].bitcast(F32).rearrange("p (s b u) -> p s b u", b=BS, u=2)
            for half in range(GROUP // 2):
                pairs_onto_partitions(
                    src[:, 2 * half : 2 * half + 2, :], dst[:, 2 * half : 2 * half + 2, :, :]
                )
            grouped_of[g] = grouped

        def quantise_group(g):
            codes = work_pool.tile([P, GROUP * BS], U32, align_bytes=64)
            scales = work_pool.tile([P, GROUP * BS], U8, align_bytes=64)
            nc.vector.quantize_mx(
                out=codes[:].bitcast(FP8X4), scales=scales[:], in_=grouped_of[g][:]
            )
            codes_of[g] = codes
            scales_of[g] = scales

        def project_group(g):
            for j in range(GROUP):
                batch = slice(j * BS, (j + 1) * BS)
                proj = proj_pool.tile([P, DP], F32)
                nc.tensor.matmul_mx(
                    out=proj[:],
                    lhsT=codes_of[g][:, batch].bitcast(FP8X4),
                    lhsT_scale=scales_of[g][:, batch],
                    rhs=wv_codes[:].bitcast(FP8X4),
                    rhs_scale=wv_scales[:],
                    start=True,
                    stop=True,
                )
                proj_of[g * GROUP + j] = proj

        def by_scalar(s):
            return s % SCALAR_EVERY == SCALAR_EVERY - 1

        attn_part = const.tile([P, DP], F32)
        nc.vector.memset(attn_part[:], 0.0)

        def pool_group(g):
            for s in range(g * GROUP, (g + 1) * GROUP):
                if by_scalar(s):
                    product = prod_pool.tile([P, DP], F32)
                    product_of[s] = product
                for h in range(H):
                    head = slice(h * NH, (h + 1) * NH)
                    if by_scalar(s):
                        nc.scalar.activation(
                            out=product[:, head],
                            in_=proj_of[s][:, head],
                            func=COPY,
                            scale=weight[:, h, s : s + 1],
                        )
                    else:
                        nc.vector.scalar_tensor_tensor(
                            out=attn_part[:, head],
                            in0=proj_of[s][:, head],
                            scalar=weight[:, h, s : s + 1],
                            in1=attn_part[:, head],
                            op0=MULT,
                            op1=ADD,
                        )

        attn_sum = sum_pool.tile([P, PACK, BS], F32)

        def add_transposed(term, first, last):
            for t in range(PACK):
                nc.tensor.matmul(
                    out=attn_sum[:, t, :],
                    lhsT=term[:, t * P : (t + 1) * P],
                    rhs=ident[:],
                    is_transpose=True,
                    start=first and t == 0,
                    stop=last and t == PACK - 1,
                )

        def add_products_of_group(g):
            for s in range(g * GROUP, (g + 1) * GROUP):
                if by_scalar(s):
                    add_transposed(product_of[s], first=(s == SCALAR_EVERY - 1), last=False)

        transpose_group(0)
        transpose_logw()
        transpose_group(1)
        for g in range(1, N_GROUPS + 3):
            if g <= N_GROUPS:
                quantise_group(g - 1)
            if g == WO_ROUND + 1:
                quantise_wo()
            if 2 <= g <= N_GROUPS + 1:
                pool_group(g - 2)
            if g + 1 < N_GROUPS:
                transpose_group(g + 1)
            if g >= 3:
                add_products_of_group(g - 3)
            if g == WO_ROUND:
                transpose_wo()
            if g <= N_GROUPS:
                project_group(g - 1)

        add_transposed(attn_part, first=False, last=True)
        attn_grouped = const.tile([P, BS, PACK], BF16, align_bytes=64)
        nc.scalar.copy(out=attn_grouped[:], in_=attn_sum[:].rearrange("p t b -> p b t"))
        attn_codes = const.tile([P, BS], U32, align_bytes=64)
        attn_scales = const.tile([P, BS], U8, align_bytes=64)
        nc.vector.quantize_mx(
            out=attn_codes[:].bitcast(FP8X4),
            scales=attn_scales[:],
            in_=attn_grouped[:].rearrange("p b t -> p (b t)"),
        )
        out_bank = flip_pool.tile([P, DO], F32, tag="flip")
        nc.tensor.matmul_mx(
            out=out_bank[:],
            lhsT=attn_codes[:].bitcast(FP8X4),
            lhsT_scale=attn_scales[:],
            rhs=wo_codes[:].bitcast(FP8X4),
            rhs_scale=wo_scales[:],
            start=True,
            stop=True,
        )
        out_rows = const.tile([P, DO], F32)
        nc.vector.tensor_copy(out=out_rows[:], in_=out_bank[:])
        nc.sync.dma_start(out=out, in_=out_rows[:])
